import numpy as np
import ml_dtypes


def mxq(x, axis, fmt="e4m3"):
    dtype, down = {"e4m3": (ml_dtypes.float8_e4m3fn, 7), "e5m2": (ml_dtypes.float8_e5m2, 14)}[fmt]
    v = np.moveaxis(np.asarray(x, np.float32).astype(ml_dtypes.bfloat16).astype(np.float64), axis, -1)
    blocks = v.reshape(v.shape[:-1] + (-1, 32))
    amax = np.abs(blocks).max(-1, keepdims=True)
    byte = np.maximum(np.where(amax > 0, np.frexp(amax)[1] - 1 + 127, 0) - down, 1)
    scale = np.exp2(byte - 127.0)
    codes = (blocks / scale).astype(np.float32).astype(dtype).astype(np.float64)
    return np.moveaxis((codes * scale).reshape(v.shape), -1, axis)


WIDE = False


def mx_kscale(k):
    if not WIDE:
        return np.ones(k)
    levels = np.array([10, -10, 5, -5, 0])
    a = np.random.permutation(np.resize(levels, k // 512 * 4)).reshape(k // 512, 4)
    idx = np.arange(k)
    return np.exp2(a[idx // 512, idx % 128 // 32])


BF16 = ml_dtypes.bfloat16


def bf(x):
    return np.asarray(x, np.float32).astype(BF16)


def f64(x):
    return np.asarray(x).astype(np.float64)


B, T, D, H, KH, F = 2, 2048, 512, 8, 2, 128
EPS = 1e-5


def layer_norm(v, g, b):
    m = v.mean(-1, keepdims=True)
    var = ((v - m) ** 2).mean(-1, keepdims=True)
    return (v - m) / np.sqrt(var + EPS) * g + b


def setup_inputs():
    s, t = mx_kscale(D), mx_kscale(D)
    return {
        "h_attn": bf(np.random.standard_normal((B, T, D)) * 0.4 * s),
        "x": bf(np.random.standard_normal((B, T, D))),
        "Wo": bf(np.random.standard_normal((D, D)) * 2.0 / np.sqrt(D) / s[:, None]),
        "bo": bf(np.random.standard_normal(D) * 0.2),
        "ln2_g": bf(1.5 + 0.3 * np.random.standard_normal(D)),
        "ln2_b": bf(0.3 + 0.3 * np.random.standard_normal(D)),
        "fln_g": bf((1.0 + 0.1 * np.random.standard_normal(D)) * t),
        "fln_b": bf(0.2 * np.random.standard_normal(D) * t),
        "W1": bf(np.random.standard_normal((D, F)) / np.sqrt(D) / t[:, None]),
        "b1": bf(np.random.standard_normal(F) * 0.3),
        "W2": bf(np.random.standard_normal((D, F)) / np.sqrt(D) / t[:, None]),
        "b2": bf(np.random.standard_normal(F) * 0.3),
    }


def reference(h_attn, x, Wo, bo, ln2_g, ln2_b, fln_g, fln_b, W1, b1, W2, b2):
    y = f64(x) + ((mxq(f64(h_attn), 2, "e4m3") @ mxq(f64(Wo), 0, "e4m3")) + f64(bo))
    r = layer_norm(y, f64(ln2_g), f64(ln2_b))
    h2q = mxq(layer_norm(r, f64(fln_g), f64(fln_b)), 2, "e4m3")
    g_pre = (h2q @ mxq(f64(W1), 0, "e4m3")) + f64(b1)
    hidden = (h2q @ mxq(f64(W2), 0, "e4m3")) + f64(b2)
    return r, g_pre, hidden

@@ -1,0 +1,328 @@
+import concourse.mybir as mybir
+from concourse.masks import make_identity
+
+F32 = mybir.dt.float32
+BF16 = mybir.dt.bfloat16
+U32 = mybir.dt.uint32
+U8 = mybir.dt.uint8
+FP8X4 = mybir.dt.float8_e4m3fn_x4
+ALU = mybir.AluOpType
+ACT = mybir.ActivationFunctionType
+
+P = 128
+PACK = 4
+D = 512
+F = 128
+TOKENS = 4096
+TILES = TOKENS // P
+PAIR = 2
+GROUP = 4
+EPS = 1e-5
+
+FLOPS = 2 * TOKENS * D * (D + 2 * F)
+
+
+def tile_transformerblock_pa_t_kernel(
+    tc, h_attn, x, Wo, bo, ln2_g, ln2_b, fln_g, fln_b, W1, b1, W2, b2, out_0, out_1, out_2
+):
+    nc = tc.nc
+
+    h_view = h_attn.flatten_outer_dims().rearrange("(p n) d -> p n d", n=TILES)
+    x_view = x.flatten_outer_dims().rearrange("(p n) d -> p n d", n=TILES)
+    r_view = out_0.flatten_outer_dims().rearrange("(p n) d -> p n d", n=TILES)
+    g_view = out_1.flatten_outer_dims().rearrange("(p n) f -> p n f", n=TILES)
+    hid_view = out_2.flatten_outer_dims().rearrange("(p n) f -> p n f", n=TILES)
+
+    with tc.tile_pool(name="const", bufs=1) as const, tc.tile_pool(
+        name="inputs", bufs=TILES // GROUP
+    ) as inputs, tc.tile_pool(name="work", bufs=3) as work, tc.tile_pool(
+        name="stats", bufs=4
+    ) as stats, tc.psum_pool(name="psum", bufs=1) as psum:
+        wo_raw = const.tile([P, PACK, D], BF16)
+        for u in range(2):
+            nc.sync.dma_start(
+                out=wo_raw[:, 2 * u : 2 * u + 2, :],
+                in_=Wo[256 * u : 256 * u + 256, :].rearrange("(q e) c -> q e c", e=2),
+            )
+        h_groups = []
+        x_groups = []
+        for g in range(TILES // GROUP):
+            h_grp = inputs.tile([P, GROUP, D], BF16, tag="h")
+            nc.sync.dma_start(out=h_grp[:], in_=h_view[:, GROUP * g : GROUP * (g + 1), :])
+            x_grp = inputs.tile([P, GROUP, D], BF16, tag="x")
+            nc.sync.dma_start(out=x_grp[:], in_=x_view[:, GROUP * g : GROUP * (g + 1), :])
+            h_groups.append(h_grp)
+            x_groups.append(x_grp)
+
+        w12_raw = const.tile([P, PACK, 2 * F], BF16)
+        nc.scalar.dma_start(out=w12_raw[:, :, 0:F], in_=W1.rearrange("(t p) f -> p t f", p=P))
+        nc.scalar.dma_start(out=w12_raw[:, :, F : 2 * F], in_=W2.rearrange("(t p) f -> p t f", p=P))
+
+        vec_rows = const.tile([P, 4, D], BF16)
+        nc.vector.memset(vec_rows[:], 0.0)
+        nc.scalar.dma_start(out=vec_rows[0:1, 0, :], in_=bo.unsqueeze(0))
+        nc.scalar.dma_start(out=vec_rows[0:1, 1, :], in_=ln2_g.unsqueeze(0))
+        nc.scalar.dma_start(out=vec_rows[0:1, 2, :], in_=ln2_b.unsqueeze(0))
+        nc.scalar.dma_start(out=vec_rows[0:1, 3, 0:F], in_=b1.unsqueeze(0))
+        nc.scalar.dma_start(out=vec_rows[0:1, 3, F : 2 * F], in_=b2.unsqueeze(0))
+        col_rows = const.tile([P, P], BF16)
+        nc.vector.memset(col_rows[:], 0.0)
+        nc.scalar.dma_start(out=col_rows[0:PACK, :], in_=fln_g.rearrange("(t p) -> t p", p=P))
+        nc.scalar.dma_start(out=col_rows[PACK : 2 * PACK, :], in_=fln_b.rearrange("(t p) -> t p", p=P))
+
+        ident_f32 = const.tile([P, P], F32)
+        make_identity(nc, ident_f32[:])
+        ident_bf16 = const.tile([P, P], BF16)
+        make_identity(nc, ident_bf16[:])
+        ones = const.tile([P, P], BF16)
+        nc.vector.memset(ones[:], 1.0)
+        eps = const.tile([P, 1], F32)
+        nc.vector.memset(eps[:], EPS)
+
+        g_bc = psum.tile([P, D], F32)
+        nc.tensor.matmul(out=g_bc[:], lhsT=ones[:], rhs=vec_rows[:, 1, :], start=True, stop=True)
+        b_bc = psum.tile([P, D], F32)
+        nc.tensor.matmul(out=b_bc[:], lhsT=ones[:], rhs=vec_rows[:, 2, :], start=True, stop=True)
+        bo_ps = psum.tile([P, D], F32, tag="acc", bufs=2)
+        nc.tensor.matmul(out=bo_ps[:], lhsT=ones[:], rhs=vec_rows[:, 0, :], start=True, stop=True)
+        bo_bc = const.tile([P, D], F32)
+        nc.vector.tensor_copy(out=bo_bc[:], in_=bo_ps[:])
+        b12_ps = psum.tile([P, D], F32, tag="acc", bufs=2)
+        nc.tensor.matmul(out=b12_ps[:], lhsT=ones[:], rhs=vec_rows[:, 3, :], start=True, stop=True)
+        b12_bc = const.tile([P, 2 * F], F32)
+        nc.vector.tensor_copy(out=b12_bc[:], in_=b12_ps[:, 0 : 2 * F])
+        cols_ps = psum.tile([P, P], BF16, tag="hT")
+        nc.tensor.transpose(cols_ps[:], col_rows[:], ident_bf16[:])
+        fln_cols = const.tile([P, 2 * PACK], F32)
+        nc.vector.tensor_copy(out=fln_cols[:], in_=cols_ps[:, 0 : 2 * PACK])
+
+        wo_grp = const.tile([P, D, PACK], BF16, align_bytes=64)
+        nc.vector.tensor_copy(out=wo_grp[:], in_=wo_raw[:].rearrange("p t c -> p c t"))
+        wo_codes = const.tile([P, D], U32, align_bytes=64)
+        wo_scales = const.tile([P, D], U8, align_bytes=64)
+        nc.vector.quantize_mx(
+            out=wo_codes[:].bitcast(FP8X4), scales=wo_scales[:], in_=wo_grp[:].rearrange("p c t -> p (c t)")
+        )
+        w12_grp = const.tile([P, 2 * F, PACK], BF16, align_bytes=64)
+        nc.vector.tensor_copy(out=w12_grp[:], in_=w12_raw[:].rearrange("p t c -> p c t"))
+        w12_codes = const.tile([P, 2 * F], U32, align_bytes=64)
+        w12_scales = const.tile([P, 2 * F], U8, align_bytes=64)
+        nc.vector.quantize_mx(
+            out=w12_codes[:].bitcast(FP8X4), scales=w12_scales[:], in_=w12_grp[:].rearrange("p c t -> p (c t)")
+        )
+
+        live = {}
+
+        def pair_of(groups, k):
+            first = (k * PAIR) % GROUP
+            return groups[(k * PAIR) // GROUP][:, first : first + PAIR, :]
+
+        def add_bias(k):
+            xb = work.tile([P, PAIR, D], F32, tag="xb", bufs=4)
+            nc.gpsimd.tensor_tensor(
+                out=xb[:],
+                in0=pair_of(x_groups, k),
+                in1=bo_bc[:].unsqueeze(1).to_broadcast([P, PAIR, D]),
+                op=ALU.add,
+            )
+            live["xb", k] = xb
+
+        def transpose_h(k):
+            hT = psum.tile([P, PAIR, 2, P], F32, tag="hT")
+            for j in range(PAIR):
+                words = pair_of(h_groups, k)[:, j, :].bitcast(F32)
+                for u in range(2):
+                    nc.tensor.transpose(hT[:, j, u, :], words[:, P * u : P * (u + 1)], ident_f32[:])
+            live["hT", k] = hT
+
+        def group_h(k):
+            h_grouped = work.tile([P, PAIR * P, PACK], BF16, tag="h_grouped", align_bytes=64)
+            nc.scalar.copy(
+                out=h_grouped[:].bitcast(F32).rearrange("p (j r) u -> p j r u", j=PAIR),
+                in_=live["hT", k][:].rearrange("p j u r -> p j r u"),
+            )
+            live["h_grouped", k] = h_grouped
+
+        def quantise(name, k):
+            codes = work.tile([P, PAIR * P], U32, tag=name + "_codes", align_bytes=64)
+            scales = work.tile([P, PAIR * P], U8, tag=name + "_scales", align_bytes=64)
+            nc.vector.quantize_mx(
+                out=codes[:].bitcast(FP8X4),
+                scales=scales[:],
+                in_=live[name + "_grouped", k][:].rearrange("p r t -> p (r t)"),
+            )
+            live[name + "_codes", k] = codes
+            live[name + "_scales", k] = scales
+
+        def multiply(name, k, j, out, w_codes, w_scales):
+            nc.tensor.matmul_mx(
+                out=out,
+                lhsT=live[name + "_codes", k][:, P * j : P * (j + 1)].bitcast(FP8X4),
+                lhsT_scale=live[name + "_scales", k][:, P * j : P * (j + 1)],
+                rhs=w_codes[:].bitcast(FP8X4),
+                rhs_scale=w_scales[:],
+                start=True,
+                stop=True,
+            )
+
+        def project(k):
+            for j in range(PAIR):
+                acc = psum.tile([P, D], F32, tag="acc", bufs=2)
+                multiply("h", k, j, acc[:], wo_codes, wo_scales)
+                live["acc", k, j] = acc
+
+        def residual(k):
+            y = work.tile([P, PAIR, D], F32, tag="y")
+            y_sum = stats.tile([P, PAIR], F32, tag="y_sum")
+            for j in range(PAIR):
+                nc.vector.scalar_tensor_tensor(
+                    out=y[:, j, :],
+                    in0=live["acc", k, j][:],
+                    scalar=1.0,
+                    in1=live["xb", k][:, j, :],
+                    op0=ALU.mult,
+                    op1=ALU.add,
+                    accum_out=y_sum[:, j : j + 1],
+                )
+            live["y", k] = y
+            live["y_sum", k] = y_sum
+
+        def spread(name, k):
+            neg_mean = stats.tile([P, PAIR], F32, tag=name + "_negmean")
+            nc.scalar.mul(out=neg_mean[:], in_=live[name + "_sum", k][:], mul=-1.0 / D)
+            sum_sq = stats.tile([P, PAIR], F32, tag=name + "_sumsq")
+            for j in range(PAIR):
+                squares = work.tile([P, D], BF16, tag="squares", bufs=4)
+                nc.scalar.activation(
+                    out=squares[:],
+                    in_=live[name, k][:, j, :],
+                    func=ACT.Square,
+                    bias=neg_mean[:, j : j + 1],
+                    scale=1.0,
+                    accum_out=sum_sq[:, j : j + 1],
+                )
+            std = stats.tile([P, PAIR], F32, tag=name + "_std")
+            nc.scalar.activation(out=std[:], in_=sum_sq[:], func=ACT.Sqrt, bias=eps[:], scale=1.0 / D)
+            live[name + "_negmean", k] = neg_mean
+            live[name + "_std", k] = std
+
+        def inverse_std(name, k):
+            rstd = stats.tile([P, PAIR], F32, tag=name + "_rstd")
+            nc.vector.reciprocal(out=rstd[:], in_=live[name + "_std", k][:])
+            return rstd
+
+        def first_norm(k):
+            rstd = inverse_std("y", k)
+            scaled = work.tile([P, PAIR, D], F32, tag="scaled", bufs=2)
+            r = work.tile([P, PAIR, D], F32, tag="r", bufs=4)
+            r_sum = stats.tile([P, PAIR], F32, tag="r_sum")
+            for j in range(PAIR):
+                nc.vector.scalar_tensor_tensor(
+                    out=scaled[:, j, :],
+                    in0=live["y", k][:, j, :],
+                    scalar=live["y_negmean", k][:, j : j + 1],
+                    in1=g_bc[:],
+                    op0=ALU.add,
+                    op1=ALU.mult,
+                )
+            for j in range(PAIR):
+                nc.vector.scalar_tensor_tensor(
+                    out=r[:, j, :],
+                    in0=scaled[:, j, :],
+                    scalar=rstd[:, j : j + 1],
+                    in1=b_bc[:],
+                    op0=ALU.mult,
+                    op1=ALU.add,
+                    accum_out=r_sum[:, j : j + 1],
+                )
+            nc.sync.dma_start(out=r_view[:, PAIR * k : PAIR * (k + 1), :], in_=r[:])
+            live["r", k] = r
+            live["r_sum", k] = r_sum
+
+        def second_norm(k):
+            rstd = inverse_std("r", k)
+            normed = work.tile([P, PAIR, D], F32, tag="normed", bufs=2)
+            for j in range(PAIR):
+                nc.vector.tensor_scalar(
+                    out=normed[:, j, :],
+                    in0=live["r", k][:, j, :],
+                    scalar1=live["r_negmean", k][:, j : j + 1],
+                    scalar2=rstd[:, j : j + 1],
+                    op0=ALU.add,
+                    op1=ALU.mult,
+                )
+            live["normed", k] = normed
+
+        def transpose_normed(k):
+            for half in range(2):
+                nT = psum.tile([P, 2, PAIR * P], F32, tag="nT%d" % half)
+                for t in range(2):
+                    cols = slice(P * (2 * half + t), P * (2 * half + t + 1))
+                    for j in range(PAIR):
+                        nc.tensor.transpose(nT[:, t, P * j : P * (j + 1)], live["normed", k][:, j, cols], ident_f32[:])
+                live["nT", k, half] = nT
+
+        def gain(k):
+            h2T = work.tile([P, PACK, PAIR * P], BF16, tag="h2T", bufs=2)
+            for t in range(PACK):
+                nc.scalar.activation(
+                    out=h2T[:, t, :],
+                    in_=live["nT", k, t // 2][:, t % 2, :],
+                    func=ACT.Identity,
+                    bias=fln_cols[:, PACK + t : PACK + t + 1],
+                    scale=fln_cols[:, t : t + 1],
+                )
+            live["h2T", k] = h2T
+
+        def group_h2(k):
+            h2_grouped = work.tile([P, PAIR * P, PACK], BF16, tag="h2_grouped", bufs=2, align_bytes=64)
+            nc.vector.tensor_copy(out=h2_grouped[:], in_=live["h2T", k][:].rearrange("p t r -> p r t"))
+            live["h2_grouped", k] = h2_grouped
+
+        def project2(k):
+            acc2 = psum.tile([P, PAIR, 2 * F], F32, tag="acc2")
+            for j in range(PAIR):
+                multiply("h2", k, j, acc2[:, j, :], w12_codes, w12_scales)
+            live["acc2", k] = acc2
+
+        def bias2(k):
+            first = (k * PAIR) % GROUP
+            if first == 0:
+                out12 = work.tile([P, 2, GROUP, F], F32, tag="out12", bufs=2)
+                live["out12"] = out12
+            out12 = live["out12"]
+            nc.vector.tensor_tensor(
+                out=out12[:, :, first : first + PAIR, :].rearrange("p w j f -> p j w f"),
+                in0=live["acc2", k][:].rearrange("p j (w f) -> p j w f", w=2),
+                in1=b12_bc[:].rearrange("p (w f) -> p w f", w=2).unsqueeze(1).to_broadcast([P, PAIR, 2, F]),
+                op=ALU.add,
+            )
+            if first + PAIR == GROUP:
+                tiles = slice(PAIR * (k + 1) - GROUP, PAIR * (k + 1))
+                nc.sync.dma_start(out=g_view[:, tiles, :], in_=out12[:, 0, :, :])
+                nc.sync.dma_start(out=hid_view[:, tiles, :], in_=out12[:, 1, :, :])
+
+        pairs = TILES // PAIR
+
+        def run(step, k, *names):
+            if 0 <= k < pairs:
+                step(*names, k)
+
+        with tc.manual_schedule():
+            for i in range(-3, pairs + 4):
+                run(residual, i)
+                run(project, i + 1)
+                run(spread, i, "y")
+                run(first_norm, i - 1)
+                run(group_h, i + 2)
+                run(transpose_h, i + 3)
+                run(spread, i - 1, "r")
+                run(second_norm, i - 2)
+                run(transpose_normed, i - 2)
+                run(gain, i - 2)
+                run(group_h2, i - 3)
+                run(quantise, i + 2, "h")
+                run(bias2, i - 4)
+                run(quantise, i - 3, "h2")
+                run(project2, i - 3)
+                run(add_bias, i + 2)

@@ -118,7 +118,7 @@ def tile_transformerblock_pa_t_kernel(
             return groups[(k * PAIR) // GROUP][:, first : first + PAIR, :]
 
         def add_bias(k):
-            xb = work.tile([P, PAIR, D], F32, tag="xb", bufs=4)
+            xb = work.tile([P, PAIR, D], F32, tag="xb", bufs=2)
             nc.gpsimd.tensor_tensor(
                 out=xb[:],
                 in0=pair_of(x_groups, k),

@@ -16,6 +16,7 @@ F = 128
 TOKENS = 4096
 TILES = TOKENS // P
 PAIR = 2
+PAIRS = TILES // PAIR
 GROUP = 4
 EPS = 1e-5
 
@@ -33,104 +34,116 @@ def tile_transformerblock_pa_t_kernel(
     g_view = out_1.flatten_outer_dims().rearrange("(p n) f -> p n f", n=TILES)
     hid_view = out_2.flatten_outer_dims().rearrange("(p n) f -> p n f", n=TILES)
 
-    with tc.tile_pool(name="const", bufs=1) as const, tc.tile_pool(
-        name="inputs", bufs=TILES // GROUP
-    ) as inputs, tc.tile_pool(name="work", bufs=3) as work, tc.tile_pool(
-        name="stats", bufs=4
-    ) as stats, tc.psum_pool(name="psum", bufs=1) as psum:
+    with tc.tile_pool(name="const", bufs=1) as const, tc.tile_pool(name="inputs", bufs=PAIRS) as inputs, tc.tile_pool(
+        name="work", bufs=3
+    ) as work, tc.tile_pool(name="stats", bufs=4) as stats, tc.psum_pool(
+        name="psum", bufs=1
+    ) as psum, tc.manual_schedule():
+        live = {}
+
+        ones = const.tile([P, P], BF16)
+        nc.vector.memset(ones[:], 1.0)
+
+        def row_plane(width, name):
+            plane = const.tile([P, width], BF16, name=name)
+            nc.vector.memset(plane[:], 0.0)
+            return plane
+
+        def spread_row(out, plane):
+            nc.tensor.matmul(out=out, lhsT=ones[:], rhs=plane[:], start=True, stop=True)
+
+        def quantise_weight(raw, width, name):
+            grouped = const.tile([P, width, PACK], BF16, name=name + "_grouped", align_bytes=64)
+            nc.vector.tensor_copy(
+                out=grouped[:].rearrange("p (c i) t -> p c t i", i=4),
+                in_=raw[:].rearrange("p t (c i) -> p c t i", i=4),
+            )
+            codes = const.tile([P, width], U32, name=name + "_codes", align_bytes=64)
+            scales = const.tile([P, width], U8, name=name + "_scales", align_bytes=64)
+            nc.vector.quantize_mx(
+                out=codes[:].bitcast(FP8X4), scales=scales[:], in_=grouped[:].rearrange("p c t -> p (c t)")
+            )
+            return codes, scales
+
+        bo_row = row_plane(D, "bo_row")
+        g_row = row_plane(D, "g_row")
+        b_row = row_plane(D, "b_row")
+        b12_row = row_plane(2 * F, "b12_row")
+        fln_rows = row_plane(P, "fln_rows")
+        eps = const.tile([P, 1], F32)
+        nc.vector.memset(eps[:], EPS)
+        nc.scalar.dma_start(out=bo_row[0:1, :], in_=bo.unsqueeze(0))
+        nc.scalar.dma_start(out=g_row[0:1, :], in_=ln2_g.unsqueeze(0))
+        nc.scalar.dma_start(out=b_row[0:1, :], in_=ln2_b.unsqueeze(0))
+
         wo_raw = const.tile([P, PACK, D], BF16)
         for u in range(2):
             nc.sync.dma_start(
                 out=wo_raw[:, 2 * u : 2 * u + 2, :],
                 in_=Wo[256 * u : 256 * u + 256, :].rearrange("(q e) c -> q e c", e=2),
             )
-        h_groups = []
-        x_groups = []
-        for g in range(TILES // GROUP):
-            h_grp = inputs.tile([P, GROUP, D], BF16, tag="h")
-            nc.sync.dma_start(out=h_grp[:], in_=h_view[:, GROUP * g : GROUP * (g + 1), :])
-            x_grp = inputs.tile([P, GROUP, D], BF16, tag="x")
-            nc.sync.dma_start(out=x_grp[:], in_=x_view[:, GROUP * g : GROUP * (g + 1), :])
-            h_groups.append(h_grp)
-            x_groups.append(x_grp)
 
+        def load_pair(k):
+            h_pair = inputs.tile([P, PAIR, D], BF16, tag="h")
+            nc.sync.dma_start(out=h_pair[:], in_=h_view[:, PAIR * k : PAIR * (k + 1), :])
+            x_pair = inputs.tile([P, PAIR, D], BF16, tag="x")
+            nc.sync.dma_start(out=x_pair[:], in_=x_view[:, PAIR * k : PAIR * (k + 1), :])
+            live["h", k] = h_pair
+            live["x", k] = x_pair
+
+        load_pair(0)
+        load_pair(1)
         w12_raw = const.tile([P, PACK, 2 * F], BF16)
-        nc.scalar.dma_start(out=w12_raw[:, :, 0:F], in_=W1.rearrange("(t p) f -> p t f", p=P))
-        nc.scalar.dma_start(out=w12_raw[:, :, F : 2 * F], in_=W2.rearrange("(t p) f -> p t f", p=P))
-
-        vec_rows = const.tile([P, 4, D], BF16)
-        nc.vector.memset(vec_rows[:], 0.0)
-        nc.scalar.dma_start(out=vec_rows[0:1, 0, :], in_=bo.unsqueeze(0))
-        nc.scalar.dma_start(out=vec_rows[0:1, 1, :], in_=ln2_g.unsqueeze(0))
-        nc.scalar.dma_start(out=vec_rows[0:1, 2, :], in_=ln2_b.unsqueeze(0))
-        nc.scalar.dma_start(out=vec_rows[0:1, 3, 0:F], in_=b1.unsqueeze(0))
-        nc.scalar.dma_start(out=vec_rows[0:1, 3, F : 2 * F], in_=b2.unsqueeze(0))
-        col_rows = const.tile([P, P], BF16)
-        nc.vector.memset(col_rows[:], 0.0)
-        nc.scalar.dma_start(out=col_rows[0:PACK, :], in_=fln_g.rearrange("(t p) -> t p", p=P))
-        nc.scalar.dma_start(out=col_rows[PACK : 2 * PACK, :], in_=fln_b.rearrange("(t p) -> t p", p=P))
+        nc.sync.dma_start(out=fln_rows[0:PACK, :], in_=fln_g.rearrange("(t p) -> t p", p=P))
+        nc.sync.dma_start(out=fln_rows[PACK : 2 * PACK, :], in_=fln_b.rearrange("(t p) -> t p", p=P))
+        nc.sync.dma_start(out=w12_raw[:, :, 0:F], in_=W1.rearrange("(t p) f -> p t f", p=P))
+        nc.sync.dma_start(out=w12_raw[:, :, F : 2 * F], in_=W2.rearrange("(t p) f -> p t f", p=P))
+        nc.sync.dma_start(out=b12_row[0:1, 0:F], in_=b1.unsqueeze(0))
+        nc.sync.dma_start(out=b12_row[0:1, F : 2 * F], in_=b2.unsqueeze(0))
+        for k in range(2, PAIRS):
+            load_pair(k)
 
         ident_f32 = const.tile([P, P], F32)
         make_identity(nc, ident_f32[:])
         ident_bf16 = const.tile([P, P], BF16)
         make_identity(nc, ident_bf16[:])
-        ones = const.tile([P, P], BF16)
-        nc.vector.memset(ones[:], 1.0)
-        eps = const.tile([P, 1], F32)
-        nc.vector.memset(eps[:], EPS)
-
-        g_bc = psum.tile([P, D], F32)
-        nc.tensor.matmul(out=g_bc[:], lhsT=ones[:], rhs=vec_rows[:, 1, :], start=True, stop=True)
-        b_bc = psum.tile([P, D], F32)
-        nc.tensor.matmul(out=b_bc[:], lhsT=ones[:], rhs=vec_rows[:, 2, :], start=True, stop=True)
-        bo_ps = psum.tile([P, D], F32, tag="acc", bufs=2)
-        nc.tensor.matmul(out=bo_ps[:], lhsT=ones[:], rhs=vec_rows[:, 0, :], start=True, stop=True)
+        bo_ps = psum.tile([P, D], F32, tag="nT1")
+        spread_row(bo_ps[:], bo_row)
         bo_bc = const.tile([P, D], F32)
-        nc.vector.tensor_copy(out=bo_bc[:], in_=bo_ps[:])
-        b12_ps = psum.tile([P, D], F32, tag="acc", bufs=2)
-        nc.tensor.matmul(out=b12_ps[:], lhsT=ones[:], rhs=vec_rows[:, 3, :], start=True, stop=True)
-        b12_bc = const.tile([P, 2 * F], F32)
-        nc.vector.tensor_copy(out=b12_bc[:], in_=b12_ps[:, 0 : 2 * F])
-        cols_ps = psum.tile([P, P], BF16, tag="hT")
-        nc.tensor.transpose(cols_ps[:], col_rows[:], ident_bf16[:])
-        fln_cols = const.tile([P, 2 * PACK], F32)
-        nc.vector.tensor_copy(out=fln_cols[:], in_=cols_ps[:, 0 : 2 * PACK])
+        nc.scalar.copy(out=bo_bc[:], in_=bo_ps[:])
+        wo_codes, wo_scales = quantise_weight(wo_raw, D, "wo")
 
-        wo_grp = const.tile([P, D, PACK], BF16, align_bytes=64)
-        nc.vector.tensor_copy(out=wo_grp[:], in_=wo_raw[:].rearrange("p t c -> p c t"))
-        wo_codes = const.tile([P, D], U32, align_bytes=64)
-        wo_scales = const.tile([P, D], U8, align_bytes=64)
-        nc.vector.quantize_mx(
-            out=wo_codes[:].bitcast(FP8X4), scales=wo_scales[:], in_=wo_grp[:].rearrange("p c t -> p (c t)")
-        )
-        w12_grp = const.tile([P, 2 * F, PACK], BF16, align_bytes=64)
-        nc.vector.tensor_copy(out=w12_grp[:], in_=w12_raw[:].rearrange("p t c -> p c t"))
-        w12_codes = const.tile([P, 2 * F], U32, align_bytes=64)
-        w12_scales = const.tile([P, 2 * F], U8, align_bytes=64)
-        nc.vector.quantize_mx(
-            out=w12_codes[:].bitcast(FP8X4), scales=w12_scales[:], in_=w12_grp[:].rearrange("p c t -> p (c t)")
-        )
-
-        live = {}
-
-        def pair_of(groups, k):
-            first = (k * PAIR) % GROUP
-            return groups[(k * PAIR) // GROUP][:, first : first + PAIR, :]
+        def late_setup():
+            g_bc = psum.tile([P, D], F32)
+            spread_row(g_bc[:], g_row)
+            b_bc = psum.tile([P, D], F32)
+            spread_row(b_bc[:], b_row)
+            b12_ps = psum.tile([P, 2 * F], F32, tag="acc2")
+            spread_row(b12_ps[:], b12_row)
+            b12_bc = const.tile([P, 2 * F], F32)
+            nc.scalar.copy(out=b12_bc[:], in_=b12_ps[:])
+            cols_ps = psum.tile([P, P], BF16, tag="nT0")
+            nc.tensor.transpose(cols_ps[:], fln_rows[:], ident_bf16[:])
+            fln_cols = const.tile([P, 2 * PACK], F32)
+            nc.scalar.copy(out=fln_cols[:], in_=cols_ps[:, 0 : 2 * PACK])
+            w12_codes, w12_scales = quantise_weight(w12_raw, 2 * F, "w12")
+            live["g_bc"] = g_bc
+            live["b_bc"] = b_bc
+            live["b12_bc"] = b12_bc
+            live["fln_cols"] = fln_cols
+            live["w12"] = (w12_codes, w12_scales)
 
         def add_bias(k):
             xb = work.tile([P, PAIR, D], F32, tag="xb", bufs=2)
             nc.gpsimd.tensor_tensor(
-                out=xb[:],
-                in0=pair_of(x_groups, k),
-                in1=bo_bc[:].unsqueeze(1).to_broadcast([P, PAIR, D]),
-                op=ALU.add,
+                out=xb[:], in0=live["x", k][:], in1=bo_bc[:].unsqueeze(1).to_broadcast([P, PAIR, D]), op=ALU.add
             )
             live["xb", k] = xb
 
         def transpose_h(k):
             hT = psum.tile([P, PAIR, 2, P], F32, tag="hT")
             for j in range(PAIR):
-                words = pair_of(h_groups, k)[:, j, :].bitcast(F32)
+                words = live["h", k][:, j, :].bitcast(F32)
                 for u in range(2):
                     nc.tensor.transpose(hT[:, j, u, :], words[:, P * u : P * (u + 1)], ident_f32[:])
             live["hT", k] = hT
@@ -209,10 +222,10 @@ def tile_transformerblock_pa_t_kernel(
         def inverse_std(name, k):
             rstd = stats.tile([P, PAIR], F32, tag=name + "_rstd")
             nc.vector.reciprocal(out=rstd[:], in_=live[name + "_std", k][:])
-            return rstd
+            live[name + "_rstd", k] = rstd
 
         def first_norm(k):
-            rstd = inverse_std("y", k)
+            inverse_std("y", k)
             scaled = work.tile([P, PAIR, D], F32, tag="scaled", bufs=2)
             r = work.tile([P, PAIR, D], F32, tag="r", bufs=4)
             r_sum = stats.tile([P, PAIR], F32, tag="r_sum")
@@ -221,7 +234,7 @@ def tile_transformerblock_pa_t_kernel(
                     out=scaled[:, j, :],
                     in0=live["y", k][:, j, :],
                     scalar=live["y_negmean", k][:, j : j + 1],
-                    in1=g_bc[:],
+                    in1=live["g_bc"][:],
                     op0=ALU.add,
                     op1=ALU.mult,
                 )
@@ -229,8 +242,8 @@ def tile_transformerblock_pa_t_kernel(
                 nc.vector.scalar_tensor_tensor(
                     out=r[:, j, :],
                     in0=scaled[:, j, :],
-                    scalar=rstd[:, j : j + 1],
-                    in1=b_bc[:],
+                    scalar=live["y_rstd", k][:, j : j + 1],
+                    in1=live["b_bc"][:],
                     op0=ALU.mult,
                     op1=ALU.add,
                     accum_out=r_sum[:, j : j + 1],
@@ -240,14 +253,13 @@ def tile_transformerblock_pa_t_kernel(
             live["r_sum", k] = r_sum
 
         def second_norm(k):
-            rstd = inverse_std("r", k)
             normed = work.tile([P, PAIR, D], F32, tag="normed", bufs=2)
             for j in range(PAIR):
-                nc.vector.tensor_scalar(
+                nc.gpsimd.tensor_scalar(
                     out=normed[:, j, :],
                     in0=live["r", k][:, j, :],
                     scalar1=live["r_negmean", k][:, j : j + 1],
-                    scalar2=rstd[:, j : j + 1],
+                    scalar2=live["r_rstd", k][:, j : j + 1],
                     op0=ALU.add,
                     op1=ALU.mult,
                 )
@@ -269,20 +281,23 @@ def tile_transformerblock_pa_t_kernel(
                     out=h2T[:, t, :],
                     in_=live["nT", k, t // 2][:, t % 2, :],
                     func=ACT.Identity,
-                    bias=fln_cols[:, PACK + t : PACK + t + 1],
-                    scale=fln_cols[:, t : t + 1],
+                    bias=live["fln_cols"][:, PACK + t : PACK + t + 1],
+                    scale=live["fln_cols"][:, t : t + 1],
                 )
             live["h2T", k] = h2T
 
         def group_h2(k):
             h2_grouped = work.tile([P, PAIR * P, PACK], BF16, tag="h2_grouped", bufs=2, align_bytes=64)
-            nc.vector.tensor_copy(out=h2_grouped[:], in_=live["h2T", k][:].rearrange("p t r -> p r t"))
+            nc.vector.tensor_copy(
+                out=h2_grouped[:].rearrange("p (c i) t -> p c t i", i=4),
+                in_=live["h2T", k][:].rearrange("p t (c i) -> p c t i", i=4),
+            )
             live["h2_grouped", k] = h2_grouped
 
         def project2(k):
             acc2 = psum.tile([P, PAIR, 2 * F], F32, tag="acc2")
             for j in range(PAIR):
-                multiply("h2", k, j, acc2[:, j, :], w12_codes, w12_scales)
+                multiply("h2", k, j, acc2[:, j, :], live["w12"][0], live["w12"][1])
             live["acc2", k] = acc2
 
         def bias2(k):
@@ -294,7 +309,7 @@ def tile_transformerblock_pa_t_kernel(
             nc.vector.tensor_tensor(
                 out=out12[:, :, first : first + PAIR, :].rearrange("p w j f -> p j w f"),
                 in0=live["acc2", k][:].rearrange("p j (w f) -> p j w f", w=2),
-                in1=b12_bc[:].rearrange("p (w f) -> p w f", w=2).unsqueeze(1).to_broadcast([P, PAIR, 2, F]),
+                in1=live["b12_bc"][:].rearrange("p (w f) -> p w f", w=2).unsqueeze(1).to_broadcast([P, PAIR, 2, F]),
                 op=ALU.add,
             )
             if first + PAIR == GROUP:
@@ -302,27 +317,27 @@ def tile_transformerblock_pa_t_kernel(
                 nc.sync.dma_start(out=g_view[:, tiles, :], in_=out12[:, 0, :, :])
                 nc.sync.dma_start(out=hid_view[:, tiles, :], in_=out12[:, 1, :, :])
 
-        pairs = TILES // PAIR
-
         def run(step, k, *names):
-            if 0 <= k < pairs:
+            if 0 <= k < PAIRS:
                 step(*names, k)
 
-        with tc.manual_schedule():
-            for i in range(-3, pairs + 4):
-                run(residual, i)
-                run(project, i + 1)
-                run(spread, i, "y")
-                run(first_norm, i - 1)
-                run(group_h, i + 2)
-                run(transpose_h, i + 3)
-                run(spread, i - 1, "r")
-                run(second_norm, i - 2)
-                run(transpose_normed, i - 2)
-                run(gain, i - 2)
-                run(group_h2, i - 3)
-                run(quantise, i + 2, "h")
-                run(bias2, i - 4)
-                run(quantise, i - 3, "h2")
-                run(project2, i - 3)
-                run(add_bias, i + 2)
+        for i in range(-3, PAIRS + 4):
+            if i == 0:
+                late_setup()
+            run(inverse_std, i - 2, "r")
+            run(second_norm, i - 2)
+            run(gain, i - 3)
+            run(residual, i)
+            run(project, i + 1)
+            run(transpose_normed, i - 2)
+            run(group_h, i + 2)
+            run(transpose_h, i + 3)
+            run(spread, i, "y")
+            run(first_norm, i - 1)
+            run(bias2, i - 4)
+            run(spread, i - 1, "r")
+            run(add_bias, i + 2)
+            run(group_h2, i - 3)
+            run(quantise, i + 2, "h")
+            run(quantise, i - 3, "h2")
+            run(project2, i - 3)

@@ -36,7 +36,7 @@ def tile_transformerblock_pa_t_kernel(
 
     with tc.tile_pool(name="const", bufs=1) as const, tc.tile_pool(name="inputs", bufs=PAIRS) as inputs, tc.tile_pool(
         name="work", bufs=3
-    ) as work, tc.tile_pool(name="stats", bufs=4) as stats, tc.psum_pool(
+    ) as work, tc.tile_pool(name="stats", bufs=5) as stats, tc.psum_pool(
         name="psum", bufs=1
     ) as psum, tc.manual_schedule():
         live = {}
@@ -227,7 +227,7 @@ def tile_transformerblock_pa_t_kernel(
         def first_norm(k):
             inverse_std("y", k)
             scaled = work.tile([P, PAIR, D], F32, tag="scaled", bufs=2)
-            r = work.tile([P, PAIR, D], F32, tag="r", bufs=4)
+            r = work.tile([P, PAIR, D], F32, tag="r", bufs=5)
             r_sum = stats.tile([P, PAIR], F32, tag="r_sum")
             for j in range(PAIR):
                 nc.vector.scalar_tensor_tensor(
@@ -321,23 +321,23 @@ def tile_transformerblock_pa_t_kernel(
             if 0 <= k < PAIRS:
                 step(*names, k)
 
-        for i in range(-3, PAIRS + 4):
+        for i in range(-3, PAIRS + 5):
             if i == 0:
                 late_setup()
-            run(inverse_std, i - 2, "r")
-            run(second_norm, i - 2)
-            run(gain, i - 3)
+            run(inverse_std, i - 3, "r")
+            run(second_norm, i - 3)
+            run(gain, i - 4)
             run(residual, i)
             run(project, i + 1)
-            run(transpose_normed, i - 2)
+            run(transpose_normed, i - 3)
             run(group_h, i + 2)
             run(transpose_h, i + 3)
             run(spread, i, "y")
             run(first_norm, i - 1)
-            run(bias2, i - 4)
+            run(bias2, i - 5)
             run(spread, i - 1, "r")
             run(add_bias, i + 2)
-            run(group_h2, i - 3)
+            run(group_h2, i - 4)
             run(quantise, i + 2, "h")
-            run(quantise, i - 3, "h2")
-            run(project2, i - 3)
+            run(quantise, i - 4, "h2")
+            run(project2, i - 4)

@@ -214,18 +214,14 @@ def tile_transformerblock_pa_t_kernel(
                     scale=1.0,
                     accum_out=sum_sq[:, j : j + 1],
                 )
-            std = stats.tile([P, PAIR], F32, tag=name + "_std")
-            nc.scalar.activation(out=std[:], in_=sum_sq[:], func=ACT.Sqrt, bias=eps[:], scale=1.0 / D)
-            live[name + "_negmean", k] = neg_mean
-            live[name + "_std", k] = std
-
-        def inverse_std(name, k):
             rstd = stats.tile([P, PAIR], F32, tag=name + "_rstd")
-            nc.vector.reciprocal(out=rstd[:], in_=live[name + "_std", k][:])
+            nc.scalar.activation(
+                out=rstd[:], in_=sum_sq[:], func=ACT.Abs_reciprocal_sqrt, bias=eps[:], scale=1.0 / D
+            )
+            live[name + "_negmean", k] = neg_mean
             live[name + "_rstd", k] = rstd
 
         def first_norm(k):
-            inverse_std("y", k)
             scaled = work.tile([P, PAIR, D], F32, tag="scaled", bufs=2)
             r = work.tile([P, PAIR, D], F32, tag="r", bufs=5)
             r_sum = stats.tile([P, PAIR], F32, tag="r_sum")
@@ -324,7 +320,6 @@ def tile_transformerblock_pa_t_kernel(
         for i in range(-3, PAIRS + 5):
             if i == 0:
                 late_setup()
-            run(inverse_std, i - 3, "r")
             run(second_norm, i - 3)
             run(gain, i - 4)
             run(residual, i)

@@ -317,22 +317,22 @@ def tile_transformerblock_pa_t_kernel(
             if 0 <= k < PAIRS:
                 step(*names, k)
 
-        for i in range(-3, PAIRS + 5):
+        for i in range(-3, PAIRS + 4):
             if i == 0:
                 late_setup()
-            run(second_norm, i - 3)
-            run(gain, i - 4)
+            run(second_norm, i - 2)
+            run(gain, i - 3)
             run(residual, i)
             run(project, i + 1)
-            run(transpose_normed, i - 3)
+            run(transpose_normed, i - 2)
             run(group_h, i + 2)
             run(transpose_h, i + 3)
             run(spread, i, "y")
             run(first_norm, i - 1)
-            run(bias2, i - 5)
+            run(bias2, i - 4)
             run(spread, i - 1, "r")
             run(add_bias, i + 2)
-            run(group_h2, i - 4)
+            run(group_h2, i - 3)
             run(quantise, i + 2, "h")
-            run(quantise, i - 4, "h2")
-            run(project2, i - 4)
+            run(quantise, i - 3, "h2")
+            run(project2, i - 3)

@@ -19,6 +19,7 @@ PAIR = 2
 PAIRS = TILES // PAIR
 GROUP = 4
 EPS = 1e-5
+SCALAR_ROWS = 160
 
 FLOPS = 2 * TOKENS * D * (D + 2 * F)
 
@@ -282,13 +283,19 @@ def tile_transformerblock_pa_t_kernel(
                 )
             live["h2T", k] = h2T
 
-        def group_h2(k):
-            h2_grouped = work.tile([P, PAIR * P, PACK], BF16, tag="h2_grouped", bufs=2, align_bytes=64)
-            nc.vector.tensor_copy(
-                out=h2_grouped[:].rearrange("p (c i) t -> p c t i", i=4),
-                in_=live["h2T", k][:].rearrange("p t (c i) -> p c t i", i=4),
+        def group_h2_part(copy, k, rows):
+            copy(
+                out=live["h2_grouped", k][:, rows, :].rearrange("p (c i) t -> p c t i", i=4),
+                in_=live["h2T", k][:, :, rows].rearrange("p t (c i) -> p c t i", i=4),
             )
+
+        def group_h2_scalar(k):
+            h2_grouped = work.tile([P, PAIR * P, PACK], BF16, tag="h2_grouped", bufs=2, align_bytes=64)
             live["h2_grouped", k] = h2_grouped
+            group_h2_part(nc.scalar.copy, k, slice(0, SCALAR_ROWS))
+
+        def group_h2_vector(k):
+            group_h2_part(nc.vector.tensor_copy, k, slice(SCALAR_ROWS, PAIR * P))
 
         def project2(k):
             acc2 = psum.tile([P, PAIR, 2 * F], F32, tag="acc2")
@@ -327,12 +334,13 @@ def tile_transformerblock_pa_t_kernel(
             run(transpose_normed, i - 2)
             run(group_h, i + 2)
             run(transpose_h, i + 3)
+            run(group_h2_scalar, i - 3)
             run(spread, i, "y")
             run(first_norm, i - 1)
             run(bias2, i - 4)
             run(spread, i - 1, "r")
             run(add_bias, i + 2)
-            run(group_h2, i - 3)
+            run(group_h2_vector, i - 3)
             run(quantise, i + 2, "h")
             run(quantise, i - 3, "h2")
             run(project2, i - 3)

@@ -19,7 +19,8 @@ PAIR = 2
 PAIRS = TILES // PAIR
 GROUP = 4
 EPS = 1e-5
-SCALAR_ROWS = 160
+SCALAR_ROWS = 128
+LAG_R = 2
 
 FLOPS = 2 * TOKENS * D * (D + 2 * F)
 
@@ -187,7 +188,6 @@ def tile_transformerblock_pa_t_kernel(
 
         def residual(k):
             y = work.tile([P, PAIR, D], F32, tag="y")
-            y_sum = stats.tile([P, PAIR], F32, tag="y_sum")
             for j in range(PAIR):
                 nc.vector.scalar_tensor_tensor(
                     out=y[:, j, :],
@@ -196,41 +196,60 @@ def tile_transformerblock_pa_t_kernel(
                     in1=live["xb", k][:, j, :],
                     op0=ALU.mult,
                     op1=ALU.add,
-                    accum_out=y_sum[:, j : j + 1],
+                    accum_out=sums(k)[:, j : j + 1],
                 )
             live["y", k] = y
-            live["y_sum", k] = y_sum
 
-        def spread(name, k):
-            neg_mean = stats.tile([P, PAIR], F32, tag=name + "_negmean")
-            nc.scalar.mul(out=neg_mean[:], in_=live[name + "_sum", k][:], mul=-1.0 / D)
-            sum_sq = stats.tile([P, PAIR], F32, tag=name + "_sumsq")
+        def sums(k):
+            if ("sums", k) not in live:
+                live["sums", k] = stats.tile([P, 2 * PAIR], F32, tag="sums", name="sums")
+            return live["sums", k]
+
+        def columns(k):
+            return slice(0 if k < PAIRS else PAIR, 2 * PAIR if k >= LAG_R else PAIR)
+
+        def means(k):
+            neg_mean = stats.tile([P, 2 * PAIR], F32, tag="negmean")
+            cols = columns(k)
+            nc.scalar.mul(out=neg_mean[:, cols], in_=sums(k)[:, cols], mul=-1.0 / D)
+            live["negmean", k] = neg_mean
+            live["sumsq", k] = stats.tile([P, 2 * PAIR], F32, tag="sumsq", name="sumsq")
+
+        def squares(name, k):
+            pair, first = (k, 0) if name == "y" else (k - LAG_R, PAIR)
+            if not 0 <= pair < PAIRS:
+                return
             for j in range(PAIR):
-                squares = work.tile([P, D], BF16, tag="squares", bufs=4)
+                unread = work.tile([P, D], BF16, tag="squares", bufs=4)
                 nc.scalar.activation(
-                    out=squares[:],
-                    in_=live[name, k][:, j, :],
+                    out=unread[:],
+                    in_=live[name, pair][:, j, :],
                     func=ACT.Square,
-                    bias=neg_mean[:, j : j + 1],
+                    bias=live["negmean", k][:, first + j : first + j + 1],
                     scale=1.0,
-                    accum_out=sum_sq[:, j : j + 1],
+                    accum_out=live["sumsq", k][:, first + j : first + j + 1],
                 )
-            rstd = stats.tile([P, PAIR], F32, tag=name + "_rstd")
+
+        def inverse_std(k):
+            rstd = stats.tile([P, 2 * PAIR], F32, tag="rstd")
+            cols = columns(k)
             nc.scalar.activation(
-                out=rstd[:], in_=sum_sq[:], func=ACT.Abs_reciprocal_sqrt, bias=eps[:], scale=1.0 / D
+                out=rstd[:, cols], in_=live["sumsq", k][:, cols], func=ACT.Abs_reciprocal_sqrt, bias=eps[:], scale=1.0 / D
             )
-            live[name + "_negmean", k] = neg_mean
-            live[name + "_rstd", k] = rstd
+            live["rstd", k] = rstd
+
+        def statistic(which, name, k, j):
+            kk, first = (k, 0) if name == "y" else (k + LAG_R, PAIR)
+            return live[which, kk][:, first + j : first + j + 1]
 
         def first_norm(k):
             scaled = work.tile([P, PAIR, D], F32, tag="scaled", bufs=2)
             r = work.tile([P, PAIR, D], F32, tag="r", bufs=5)
-            r_sum = stats.tile([P, PAIR], F32, tag="r_sum")
             for j in range(PAIR):
                 nc.vector.scalar_tensor_tensor(
                     out=scaled[:, j, :],
                     in0=live["y", k][:, j, :],
-                    scalar=live["y_negmean", k][:, j : j + 1],
+                    scalar=statistic("negmean", "y", k, j),
                     in1=live["g_bc"][:],
                     op0=ALU.add,
                     op1=ALU.mult,
@@ -239,15 +258,14 @@ def tile_transformerblock_pa_t_kernel(
                 nc.vector.scalar_tensor_tensor(
                     out=r[:, j, :],
                     in0=scaled[:, j, :],
-                    scalar=live["y_rstd", k][:, j : j + 1],
+                    scalar=statistic("rstd", "y", k, j),
                     in1=live["b_bc"][:],
                     op0=ALU.mult,
                     op1=ALU.add,
-                    accum_out=r_sum[:, j : j + 1],
+                    accum_out=sums(k + LAG_R)[:, PAIR + j : PAIR + j + 1],
                 )
             nc.sync.dma_start(out=r_view[:, PAIR * k : PAIR * (k + 1), :], in_=r[:])
             live["r", k] = r
-            live["r_sum", k] = r_sum
 
         def second_norm(k):
             normed = work.tile([P, PAIR, D], F32, tag="normed", bufs=2)
@@ -255,8 +273,8 @@ def tile_transformerblock_pa_t_kernel(
                 nc.gpsimd.tensor_scalar(
                     out=normed[:, j, :],
                     in0=live["r", k][:, j, :],
-                    scalar1=live["r_negmean", k][:, j : j + 1],
-                    scalar2=live["r_rstd", k][:, j : j + 1],
+                    scalar1=statistic("negmean", "r", k, j),
+                    scalar2=statistic("rstd", "r", k, j),
                     op0=ALU.add,
                     op1=ALU.mult,
                 )
@@ -320,27 +338,29 @@ def tile_transformerblock_pa_t_kernel(
                 nc.sync.dma_start(out=g_view[:, tiles, :], in_=out12[:, 0, :, :])
                 nc.sync.dma_start(out=hid_view[:, tiles, :], in_=out12[:, 1, :, :])
 
-        def run(step, k, *names):
-            if 0 <= k < PAIRS:
+        def run(step, k, *names, end=PAIRS):
+            if 0 <= k < end:
                 step(*names, k)
 
-        for i in range(-3, PAIRS + 4):
+        for i in range(-3, PAIRS + 5):
             if i == 0:
                 late_setup()
-            run(second_norm, i - 2)
-            run(gain, i - 3)
+            run(second_norm, i - 3)
             run(residual, i)
-            run(project, i + 1)
-            run(transpose_normed, i - 2)
+            run(gain, i - 4)
             run(group_h, i + 2)
+            run(means, i, end=PAIRS + LAG_R)
+            run(group_h2_scalar, i - 4)
+            run(squares, i, "r", end=PAIRS + LAG_R)
+            run(squares, i, "y", end=PAIRS + LAG_R)
+            run(inverse_std, i, end=PAIRS + LAG_R)
+            run(project, i + 1)
             run(transpose_h, i + 3)
-            run(group_h2_scalar, i - 3)
-            run(spread, i, "y")
+            run(transpose_normed, i - 3)
             run(first_norm, i - 1)
-            run(bias2, i - 4)
-            run(spread, i - 1, "r")
+            run(bias2, i - 5)
             run(add_bias, i + 2)
-            run(group_h2_vector, i - 3)
+            run(group_h2_vector, i - 4)
             run(quantise, i + 2, "h")
-            run(quantise, i - 3, "h2")
-            run(project2, i - 3)
+            run(quantise, i - 4, "h2")
+            run(project2, i - 4)

@@ -20,6 +20,7 @@ PAIRS = TILES // PAIR
 GROUP = 4
 EPS = 1e-5
 SCALAR_ROWS = 128
+WO_SPLIT = 320
 LAG_R = 2
 
 FLOPS = 2 * TOKENS * D * (D + 2 * F)
@@ -41,10 +42,10 @@ def tile_transformerblock_pa_t_kernel(
     ) as work, tc.tile_pool(name="stats", bufs=5) as stats, tc.psum_pool(
         name="psum", bufs=1
     ) as psum, tc.manual_schedule():
+        scalar_rows = slice(0, SCALAR_ROWS)
+        vector_rows = slice(SCALAR_ROWS, PAIR * P)
+        all_rows = slice(0, PAIR * P)
         live = {}
-
-        ones = const.tile([P, P], BF16)
-        nc.vector.memset(ones[:], 1.0)
 
         def row_plane(width, name):
             plane = const.tile([P, width], BF16, name=name)
@@ -54,12 +55,13 @@ def tile_transformerblock_pa_t_kernel(
         def spread_row(out, plane):
             nc.tensor.matmul(out=out, lhsT=ones[:], rhs=plane[:], start=True, stop=True)
 
-        def quantise_weight(raw, width, name):
-            grouped = const.tile([P, width, PACK], BF16, name=name + "_grouped", align_bytes=64)
-            nc.vector.tensor_copy(
-                out=grouped[:].rearrange("p (c i) t -> p c t i", i=4),
-                in_=raw[:].rearrange("p t (c i) -> p c t i", i=4),
+        def group_weight(copy, grouped, raw, cols):
+            copy(
+                out=grouped[:, cols, :].rearrange("p (c i) t -> p c t i", i=4),
+                in_=raw[:, :, cols].rearrange("p t (c i) -> p c t i", i=4),
             )
+
+        def quantise_weight(grouped, width, name):
             codes = const.tile([P, width], U32, name=name + "_codes", align_bytes=64)
             scales = const.tile([P, width], U8, name=name + "_scales", align_bytes=64)
             nc.vector.quantize_mx(
@@ -67,17 +69,29 @@ def tile_transformerblock_pa_t_kernel(
             )
             return codes, scales
 
+        eps = const.tile([P, 1], F32)
+        nc.vector.memset(eps[:], EPS)
         bo_row = row_plane(D, "bo_row")
+        warm = const.tile([P, 1], F32)
+        nc.scalar.activation(out=warm[:], in_=eps[:], func=ACT.Abs_reciprocal_sqrt, bias=eps[:], scale=1.0)
+        ones = const.tile([P, P], BF16)
+        nc.vector.memset(ones[:], 1.0)
         g_row = row_plane(D, "g_row")
         b_row = row_plane(D, "b_row")
         b12_row = row_plane(2 * F, "b12_row")
         fln_rows = row_plane(P, "fln_rows")
-        eps = const.tile([P, 1], F32)
-        nc.vector.memset(eps[:], EPS)
-        nc.scalar.dma_start(out=bo_row[0:1, :], in_=bo.unsqueeze(0))
-        nc.scalar.dma_start(out=g_row[0:1, :], in_=ln2_g.unsqueeze(0))
-        nc.scalar.dma_start(out=b_row[0:1, :], in_=ln2_b.unsqueeze(0))
+        ident_f32 = const.tile([P, P], F32)
+        make_identity(nc, ident_f32[:])
+        ident_bf16 = const.tile([P, P], BF16)
+        make_identity(nc, ident_bf16[:])
 
+        def load(name, view, k):
+            tile = inputs.tile([P, PAIR, D], BF16, tag=name)
+            nc.sync.dma_start(out=tile[:], in_=view[:, PAIR * k : PAIR * (k + 1), :])
+            live[name, k] = tile
+
+        load("h", h_view, 0)
+        nc.sync.dma_start(out=bo_row[0:1, :], in_=bo.unsqueeze(0))
         wo_raw = const.tile([P, PACK, D], BF16)
         for u in range(2):
             nc.sync.dma_start(
@@ -85,16 +99,13 @@ def tile_transformerblock_pa_t_kernel(
                 in_=Wo[256 * u : 256 * u + 256, :].rearrange("(q e) c -> q e c", e=2),
             )
 
-        def load_pair(k):
-            h_pair = inputs.tile([P, PAIR, D], BF16, tag="h")
-            nc.sync.dma_start(out=h_pair[:], in_=h_view[:, PAIR * k : PAIR * (k + 1), :])
-            x_pair = inputs.tile([P, PAIR, D], BF16, tag="x")
-            nc.sync.dma_start(out=x_pair[:], in_=x_view[:, PAIR * k : PAIR * (k + 1), :])
-            live["h", k] = h_pair
-            live["x", k] = x_pair
-
-        load_pair(0)
-        load_pair(1)
+        load("x", x_view, 0)
+        load("h", h_view, 1)
+        load("x", x_view, 1)
+        nc.sync.dma_start(out=g_row[0:1, :], in_=ln2_g.unsqueeze(0))
+        nc.sync.dma_start(out=b_row[0:1, :], in_=ln2_b.unsqueeze(0))
+        load("h", h_view, 2)
+        load("x", x_view, 2)
         w12_raw = const.tile([P, PACK, 2 * F], BF16)
         nc.sync.dma_start(out=fln_rows[0:PACK, :], in_=fln_g.rearrange("(t p) -> t p", p=P))
         nc.sync.dma_start(out=fln_rows[PACK : 2 * PACK, :], in_=fln_b.rearrange("(t p) -> t p", p=P))
@@ -102,24 +113,24 @@ def tile_transformerblock_pa_t_kernel(
         nc.sync.dma_start(out=w12_raw[:, :, F : 2 * F], in_=W2.rearrange("(t p) f -> p t f", p=P))
         nc.sync.dma_start(out=b12_row[0:1, 0:F], in_=b1.unsqueeze(0))
         nc.sync.dma_start(out=b12_row[0:1, F : 2 * F], in_=b2.unsqueeze(0))
-        for k in range(2, PAIRS):
-            load_pair(k)
+        for k in range(3, PAIRS):
+            load("h", h_view, k)
+            load("x", x_view, k)
 
-        ident_f32 = const.tile([P, P], F32)
-        make_identity(nc, ident_f32[:])
-        ident_bf16 = const.tile([P, P], BF16)
-        make_identity(nc, ident_bf16[:])
         bo_ps = psum.tile([P, D], F32, tag="nT1")
         spread_row(bo_ps[:], bo_row)
         bo_bc = const.tile([P, D], F32)
-        nc.scalar.copy(out=bo_bc[:], in_=bo_ps[:])
-        wo_codes, wo_scales = quantise_weight(wo_raw, D, "wo")
+        wo_grouped = const.tile([P, D, PACK], BF16, align_bytes=64)
 
-        def late_setup():
+        def spread_ln2():
             g_bc = psum.tile([P, D], F32)
             spread_row(g_bc[:], g_row)
             b_bc = psum.tile([P, D], F32)
             spread_row(b_bc[:], b_row)
+            live["g_bc"] = g_bc
+            live["b_bc"] = b_bc
+
+        def late_setup():
             b12_ps = psum.tile([P, 2 * F], F32, tag="acc2")
             spread_row(b12_ps[:], b12_row)
             b12_bc = const.tile([P, 2 * F], F32)
@@ -128,18 +139,19 @@ def tile_transformerblock_pa_t_kernel(
             nc.tensor.transpose(cols_ps[:], fln_rows[:], ident_bf16[:])
             fln_cols = const.tile([P, 2 * PACK], F32)
             nc.scalar.copy(out=fln_cols[:], in_=cols_ps[:, 0 : 2 * PACK])
-            w12_codes, w12_scales = quantise_weight(w12_raw, 2 * F, "w12")
-            live["g_bc"] = g_bc
-            live["b_bc"] = b_bc
+            w12_grouped = const.tile([P, 2 * F, PACK], BF16, align_bytes=64)
+            group_weight(nc.scalar.copy, w12_grouped, w12_raw, slice(0, 2 * F))
+            live["w12_grouped"] = w12_grouped
             live["b12_bc"] = b12_bc
             live["fln_cols"] = fln_cols
-            live["w12"] = (w12_codes, w12_scales)
 
-        def add_bias(k):
+        def quantise_w12():
+            live["w12"] = quantise_weight(live["w12_grouped"], 2 * F, "w12")
+
+        def add_bias(engine, bias, k):
             xb = work.tile([P, PAIR, D], F32, tag="xb", bufs=2)
-            nc.gpsimd.tensor_tensor(
-                out=xb[:], in0=live["x", k][:], in1=bo_bc[:].unsqueeze(1).to_broadcast([P, PAIR, D]), op=ALU.add
-            )
+            for j in range(PAIR):
+                engine.tensor_tensor(out=xb[:, j, :], in0=live["x", k][:, j, :], in1=bias[:], op=ALU.add)
             live["xb", k] = xb
 
         def transpose_h(k):
@@ -183,7 +195,7 @@ def tile_transformerblock_pa_t_kernel(
         def project(k):
             for j in range(PAIR):
                 acc = psum.tile([P, D], F32, tag="acc", bufs=2)
-                multiply("h", k, j, acc[:], wo_codes, wo_scales)
+                multiply("h", k, j, acc[:], live["wo"][0], live["wo"][1])
                 live["acc", k, j] = acc
 
         def residual(k):
@@ -267,10 +279,10 @@ def tile_transformerblock_pa_t_kernel(
             nc.sync.dma_start(out=r_view[:, PAIR * k : PAIR * (k + 1), :], in_=r[:])
             live["r", k] = r
 
-        def second_norm(k):
+        def second_norm(engine, k):
             normed = work.tile([P, PAIR, D], F32, tag="normed", bufs=2)
             for j in range(PAIR):
-                nc.gpsimd.tensor_scalar(
+                engine.tensor_scalar(
                     out=normed[:, j, :],
                     in0=live["r", k][:, j, :],
                     scalar1=statistic("negmean", "r", k, j),
@@ -301,19 +313,15 @@ def tile_transformerblock_pa_t_kernel(
                 )
             live["h2T", k] = h2T
 
-        def group_h2_part(copy, k, rows):
+        def group_h2(copy, rows, k):
+            if ("h2_grouped", k) not in live:
+                live["h2_grouped", k] = work.tile(
+                    [P, PAIR * P, PACK], BF16, tag="h2_grouped", name="h2_grouped", bufs=2, align_bytes=64
+                )
             copy(
                 out=live["h2_grouped", k][:, rows, :].rearrange("p (c i) t -> p c t i", i=4),
                 in_=live["h2T", k][:, :, rows].rearrange("p t (c i) -> p c t i", i=4),
             )
-
-        def group_h2_scalar(k):
-            h2_grouped = work.tile([P, PAIR * P, PACK], BF16, tag="h2_grouped", bufs=2, align_bytes=64)
-            live["h2_grouped", k] = h2_grouped
-            group_h2_part(nc.scalar.copy, k, slice(0, SCALAR_ROWS))
-
-        def group_h2_vector(k):
-            group_h2_part(nc.vector.tensor_copy, k, slice(SCALAR_ROWS, PAIR * P))
 
         def project2(k):
             acc2 = psum.tile([P, PAIR, 2 * F], F32, tag="acc2")
@@ -338,29 +346,81 @@ def tile_transformerblock_pa_t_kernel(
                 nc.sync.dma_start(out=g_view[:, tiles, :], in_=out12[:, 0, :, :])
                 nc.sync.dma_start(out=hid_view[:, tiles, :], in_=out12[:, 1, :, :])
 
-        def run(step, k, *names, end=PAIRS):
-            if 0 <= k < end:
-                step(*names, k)
+        def run(step, k, *args):
+            if 0 <= k < PAIRS:
+                step(*args, k)
 
-        for i in range(-3, PAIRS + 5):
-            if i == 0:
+        transpose_h(0)
+        group_h(0)
+        group_weight(nc.vector.tensor_copy, wo_grouped, wo_raw, slice(0, WO_SPLIT))
+        group_weight(nc.scalar.copy, wo_grouped, wo_raw, slice(WO_SPLIT, D))
+        transpose_h(1)
+        quantise("h", 0)
+        live["wo"] = quantise_weight(wo_grouped, D, "wo")
+        nc.scalar.copy(out=bo_bc[:], in_=bo_ps[:])
+        add_bias(nc.vector, bo_ps, 0)
+        add_bias(nc.gpsimd, bo_bc, 1)
+        group_h(1)
+        project(0)
+        quantise("h", 1)
+        spread_ln2()
+        transpose_h(2)
+        for i in range(PAIRS):
+            if i == 2:
                 late_setup()
-            run(second_norm, i - 3)
+            if i == 3:
+                quantise_w12()
+            run(second_norm, i - 3, nc.gpsimd)
             run(residual, i)
             run(gain, i - 4)
             run(group_h, i + 2)
-            run(means, i, end=PAIRS + LAG_R)
-            run(group_h2_scalar, i - 4)
-            run(squares, i, "r", end=PAIRS + LAG_R)
-            run(squares, i, "y", end=PAIRS + LAG_R)
-            run(inverse_std, i, end=PAIRS + LAG_R)
+            run(means, i)
+            run(group_h2, i - 4, nc.scalar.copy, scalar_rows)
+            run(squares, i, "r")
+            run(squares, i, "y")
+            run(inverse_std, i)
             run(project, i + 1)
             run(transpose_h, i + 3)
             run(transpose_normed, i - 3)
             run(first_norm, i - 1)
             run(bias2, i - 5)
-            run(add_bias, i + 2)
-            run(group_h2_vector, i - 4)
+            run(add_bias, i + 2, nc.gpsimd, bo_bc)
+            run(group_h2, i - 4, nc.vector.tensor_copy, vector_rows)
             run(quantise, i + 2, "h")
             run(quantise, i - 4, "h2")
             run(project2, i - 4)
+        n = PAIRS
+        second_norm(nc.gpsimd, n - 3)
+        gain(n - 4)
+        first_norm(n - 1)
+        transpose_normed(n - 3)
+        means(n)
+        squares("r", n)
+        inverse_std(n)
+        group_h2(nc.vector.tensor_copy, all_rows, n - 4)
+        bias2(n - 5)
+        quantise("h2", n - 4)
+        project2(n - 4)
+        gain(n - 3)
+        means(n + 1)
+        squares("r", n + 1)
+        inverse_std(n + 1)
+        second_norm(nc.vector, n - 2)
+        transpose_normed(n - 2)
+        group_h2(nc.vector.tensor_copy, all_rows, n - 3)
+        bias2(n - 4)
+        quantise("h2", n - 3)
+        project2(n - 3)
+        gain(n - 2)
+        second_norm(nc.vector, n - 1)
+        transpose_normed(n - 1)
+        group_h2(nc.vector.tensor_copy, all_rows, n - 2)
+        bias2(n - 3)
+        quantise("h2", n - 2)
+        project2(n - 2)
+        gain(n - 1)
+        group_h2(nc.vector.tensor_copy, all_rows, n - 1)
+        bias2(n - 2)
+        quantise("h2", n - 1)
+        project2(n - 1)
+        bias2(n - 1)

@@ -150,8 +150,13 @@ def tile_transformerblock_pa_t_kernel(
 
         def add_bias(engine, bias, k):
             xb = work.tile([P, PAIR, D], F32, tag="xb", bufs=2)
-            for j in range(PAIR):
-                engine.tensor_tensor(out=xb[:, j, :], in0=live["x", k][:, j, :], in1=bias[:], op=ALU.add)
+            if engine is nc.vector:
+                for j in range(PAIR):
+                    engine.tensor_tensor(out=xb[:, j, :], in0=live["x", k][:, j, :], in1=bias[:], op=ALU.add)
+            else:
+                engine.tensor_tensor(
+                    out=xb[:], in0=live["x", k][:], in1=bias[:].unsqueeze(1).to_broadcast([P, PAIR, D]), op=ALU.add
+                )
             live["xb", k] = xb
 
         def transpose_h(k):

@@ -1,6 +1,8 @@
 import concourse.mybir as mybir
 from concourse.masks import make_identity
 
+ACC_BANKS = {"acc": 2, "acc2": 1}
+
 F32 = mybir.dt.float32
 BF16 = mybir.dt.bfloat16
 U32 = mybir.dt.uint32
@@ -19,7 +21,7 @@ PAIR = 2
 PAIRS = TILES // PAIR
 GROUP = 4
 EPS = 1e-5
-SCALAR_ROWS = 128
+SCALAR_ROWS = 160
 WO_SPLIT = 320
 LAG_R = 2
 
@@ -131,7 +133,7 @@ def tile_transformerblock_pa_t_kernel(
             live["b_bc"] = b_bc
 
         def late_setup():
-            b12_ps = psum.tile([P, 2 * F], F32, tag="acc2")
+            b12_ps = psum.tile([P, 2 * F], F32, tag="acc2", bufs=ACC_BANKS["acc2"])
             spread_row(b12_ps[:], b12_row)
             b12_bc = const.tile([P, 2 * F], F32)
             nc.scalar.copy(out=b12_bc[:], in_=b12_ps[:])
@@ -150,13 +152,9 @@ def tile_transformerblock_pa_t_kernel(
 
         def add_bias(engine, bias, k):
             xb = work.tile([P, PAIR, D], F32, tag="xb", bufs=2)
-            if engine is nc.vector:
-                for j in range(PAIR):
-                    engine.tensor_tensor(out=xb[:, j, :], in0=live["x", k][:, j, :], in1=bias[:], op=ALU.add)
-            else:
-                engine.tensor_tensor(
-                    out=xb[:], in0=live["x", k][:], in1=bias[:].unsqueeze(1).to_broadcast([P, PAIR, D]), op=ALU.add
-                )
+            engine.tensor_tensor(
+                out=xb[:], in0=live["x", k][:], in1=bias[:].unsqueeze(1).to_broadcast([P, PAIR, D]), op=ALU.add
+            )
             live["xb", k] = xb
 
         def transpose_h(k):
@@ -175,16 +173,19 @@ def tile_transformerblock_pa_t_kernel(
             )
             live["h_grouped", k] = h_grouped
 
-        def quantise(name, k):
-            codes = work.tile([P, PAIR * P], U32, tag=name + "_codes", align_bytes=64)
-            scales = work.tile([P, PAIR * P], U8, tag=name + "_scales", align_bytes=64)
+        def quantise(name, k, rows=all_rows):
+            if (name + "_codes", k) not in live:
+                live[name + "_codes", k] = work.tile(
+                    [P, PAIR * P], U32, tag=name + "_codes", name=name + "_codes", align_bytes=64
+                )
+                live[name + "_scales", k] = work.tile(
+                    [P, PAIR * P], U8, tag=name + "_scales", name=name + "_scales", align_bytes=64
+                )
             nc.vector.quantize_mx(
-                out=codes[:].bitcast(FP8X4),
-                scales=scales[:],
-                in_=live[name + "_grouped", k][:].rearrange("p r t -> p (r t)"),
+                out=live[name + "_codes", k][:, rows].bitcast(FP8X4),
+                scales=live[name + "_scales", k][:, rows],
+                in_=live[name + "_grouped", k][:, rows, :].rearrange("p r t -> p (r t)"),
             )
-            live[name + "_codes", k] = codes
-            live[name + "_scales", k] = scales
 
         def multiply(name, k, j, out, w_codes, w_scales):
             nc.tensor.matmul_mx(
@@ -199,7 +200,7 @@ def tile_transformerblock_pa_t_kernel(
 
         def project(k):
             for j in range(PAIR):
-                acc = psum.tile([P, D], F32, tag="acc", bufs=2)
+                acc = psum.tile([P, D], F32, tag="acc", bufs=ACC_BANKS["acc"])
                 multiply("h", k, j, acc[:], live["wo"][0], live["wo"][1])
                 live["acc", k, j] = acc
 
@@ -306,17 +307,17 @@ def tile_transformerblock_pa_t_kernel(
                         nc.tensor.transpose(nT[:, t, P * j : P * (j + 1)], live["normed", k][:, j, cols], ident_f32[:])
                 live["nT", k, half] = nT
 
-        def gain(k):
-            h2T = work.tile([P, PACK, PAIR * P], BF16, tag="h2T", bufs=2)
-            for t in range(PACK):
+        def gain(k, planes=range(PACK), cols=all_rows):
+            if ("h2T", k) not in live:
+                live["h2T", k] = work.tile([P, PACK, PAIR * P], BF16, tag="h2T", name="h2T", bufs=2)
+            for t in planes:
                 nc.scalar.activation(
-                    out=h2T[:, t, :],
-                    in_=live["nT", k, t // 2][:, t % 2, :],
+                    out=live["h2T", k][:, t, cols],
+                    in_=live["nT", k, t // 2][:, t % 2, cols],
                     func=ACT.Identity,
                     bias=live["fln_cols"][:, PACK + t : PACK + t + 1],
                     scale=live["fln_cols"][:, t : t + 1],
                 )
-            live["h2T", k] = h2T
 
         def group_h2(copy, rows, k):
             if ("h2_grouped", k) not in live:
@@ -328,28 +329,28 @@ def tile_transformerblock_pa_t_kernel(
                 in_=live["h2T", k][:, :, rows].rearrange("p t (c i) -> p c t i", i=4),
             )
 
-        def project2(k):
-            acc2 = psum.tile([P, PAIR, 2 * F], F32, tag="acc2")
-            for j in range(PAIR):
-                multiply("h2", k, j, acc2[:, j, :], live["w12"][0], live["w12"][1])
-            live["acc2", k] = acc2
+        def project2(k, tiles=range(PAIR), tag="acc2"):
+            if ("acc2", k) not in live:
+                live["acc2", k] = psum.tile([P, PAIR, 2 * F], F32, tag=tag, name="acc2_" + tag, bufs=ACC_BANKS[tag])
+            for j in tiles:
+                multiply("h2", k, j, live["acc2", k][:, j, :], live["w12"][0], live["w12"][1])
 
-        def bias2(k):
+        def bias2(k, tiles=range(PAIR)):
             first = (k * PAIR) % GROUP
-            if first == 0:
-                out12 = work.tile([P, 2, GROUP, F], F32, tag="out12", bufs=2)
-                live["out12"] = out12
+            if first == 0 and tiles[0] == 0:
+                live["out12"] = work.tile([P, 2, GROUP, F], F32, tag="out12", name="out12", bufs=2)
             out12 = live["out12"]
+            own = slice(tiles[0], tiles[-1] + 1)
             nc.vector.tensor_tensor(
-                out=out12[:, :, first : first + PAIR, :].rearrange("p w j f -> p j w f"),
-                in0=live["acc2", k][:].rearrange("p j (w f) -> p j w f", w=2),
-                in1=live["b12_bc"][:].rearrange("p (w f) -> p w f", w=2).unsqueeze(1).to_broadcast([P, PAIR, 2, F]),
+                out=out12[:, :, first + tiles[0] : first + tiles[-1] + 1, :].rearrange("p w j f -> p j w f"),
+                in0=live["acc2", k][:, own, :].rearrange("p j (w f) -> p j w f", w=2),
+                in1=live["b12_bc"][:].rearrange("p (w f) -> p w f", w=2).unsqueeze(1).to_broadcast([P, len(tiles), 2, F]),
                 op=ALU.add,
             )
-            if first + PAIR == GROUP:
-                tiles = slice(PAIR * (k + 1) - GROUP, PAIR * (k + 1))
-                nc.sync.dma_start(out=g_view[:, tiles, :], in_=out12[:, 0, :, :])
-                nc.sync.dma_start(out=hid_view[:, tiles, :], in_=out12[:, 1, :, :])
+            if first + tiles[-1] + 1 == GROUP:
+                group = slice(PAIR * (k + 1) - GROUP, PAIR * (k + 1))
+                nc.sync.dma_start(out=g_view[:, group, :], in_=out12[:, 0, :, :])
+                nc.sync.dma_start(out=hid_view[:, group, :], in_=out12[:, 1, :, :])
 
         def run(step, k, *args):
             if 0 <= k < PAIRS:
@@ -367,7 +368,6 @@ def tile_transformerblock_pa_t_kernel(
         add_bias(nc.gpsimd, bo_bc, 1)
         group_h(1)
         project(0)
-        quantise("h", 1)
         spread_ln2()
         transpose_h(2)
         for i in range(PAIRS):
@@ -377,55 +377,65 @@ def tile_transformerblock_pa_t_kernel(
                 quantise_w12()
             run(second_norm, i - 3, nc.gpsimd)
             run(residual, i)
-            run(gain, i - 4)
+            if i <= 2:
+                quantise("h", i + 1)
+            if 0 <= i - 4:
+                gain(i - 4, range(1, PACK))
             run(group_h, i + 2)
             run(means, i)
             run(group_h2, i - 4, nc.scalar.copy, scalar_rows)
             run(squares, i, "r")
             run(squares, i, "y")
-            run(inverse_std, i)
             run(project, i + 1)
             run(transpose_h, i + 3)
             run(transpose_normed, i - 3)
+            if 0 <= i - 3:
+                gain(i - 3, range(0, 1))
+            run(inverse_std, i)
             run(first_norm, i - 1)
             run(bias2, i - 5)
             run(add_bias, i + 2, nc.gpsimd, bo_bc)
             run(group_h2, i - 4, nc.vector.tensor_copy, vector_rows)
-            run(quantise, i + 2, "h")
+            if i >= 2:
+                run(quantise, i + 2, "h")
             run(quantise, i - 4, "h2")
             run(project2, i - 4)
         n = PAIRS
+        means(n)
         second_norm(nc.gpsimd, n - 3)
-        gain(n - 4)
+        gain(n - 4, range(1, PACK))
         first_norm(n - 1)
         transpose_normed(n - 3)
-        means(n)
         squares("r", n)
-        inverse_std(n)
         group_h2(nc.vector.tensor_copy, all_rows, n - 4)
         bias2(n - 5)
         quantise("h2", n - 4)
         project2(n - 4)
         gain(n - 3)
+        inverse_std(n)
         means(n + 1)
         squares("r", n + 1)
         inverse_std(n + 1)
         second_norm(nc.vector, n - 2)
         transpose_normed(n - 2)
         group_h2(nc.vector.tensor_copy, all_rows, n - 3)
+        second_norm(nc.vector, n - 1)
+        gain(n - 2)
+        transpose_normed(n - 1)
         bias2(n - 4)
         quantise("h2", n - 3)
-        project2(n - 3)
-        gain(n - 2)
-        second_norm(nc.vector, n - 1)
-        transpose_normed(n - 1)
+        project2(n - 3, tag="acc")
+        gain(n - 1, cols=slice(0, P))
+        gain(n - 1, cols=slice(P, 2 * P))
         group_h2(nc.vector.tensor_copy, all_rows, n - 2)
-        bias2(n - 3)
         quantise("h2", n - 2)
-        project2(n - 2)
-        gain(n - 1)
-        group_h2(nc.vector.tensor_copy, all_rows, n - 1)
+        project2(n - 2, tag="acc")
+        group_h2(nc.vector.tensor_copy, slice(0, P), n - 1)
+        group_h2(nc.vector.tensor_copy, slice(P, 2 * P), n - 1)
+        quantise("h2", n - 1, slice(0, P))
+        project2(n - 1, range(0, 1))
+        quantise("h2", n - 1, slice(P, 2 * P))
+        project2(n - 1, range(1, 2))
+        bias2(n - 3)
         bias2(n - 2)
-        quantise("h2", n - 1)
-        project2(n - 1)
         bias2(n - 1)

import concourse.mybir as mybir
from concourse.masks import make_identity

ACC_BANKS = {"acc": 2, "acc2": 1}

F32 = mybir.dt.float32
BF16 = mybir.dt.bfloat16
U32 = mybir.dt.uint32
U8 = mybir.dt.uint8
FP8X4 = mybir.dt.float8_e4m3fn_x4
ALU = mybir.AluOpType
ACT = mybir.ActivationFunctionType

P = 128
PACK = 4
D = 512
F = 128
TOKENS = 4096
TILES = TOKENS // P
PAIR = 2
PAIRS = TILES // PAIR
GROUP = 4
EPS = 1e-5
SCALAR_ROWS = 160
WO_SPLIT = 320
LAG_R = 2

FLOPS = 2 * TOKENS * D * (D + 2 * F)


def tile_transformerblock_pa_t_kernel(
    tc, h_attn, x, Wo, bo, ln2_g, ln2_b, fln_g, fln_b, W1, b1, W2, b2, out_0, out_1, out_2
):
    nc = tc.nc

    h_view = h_attn.flatten_outer_dims().rearrange("(p n) d -> p n d", n=TILES)
    x_view = x.flatten_outer_dims().rearrange("(p n) d -> p n d", n=TILES)
    r_view = out_0.flatten_outer_dims().rearrange("(p n) d -> p n d", n=TILES)
    g_view = out_1.flatten_outer_dims().rearrange("(p n) f -> p n f", n=TILES)
    hid_view = out_2.flatten_outer_dims().rearrange("(p n) f -> p n f", n=TILES)

    with tc.tile_pool(name="const", bufs=1) as const, tc.tile_pool(name="inputs", bufs=PAIRS) as inputs, tc.tile_pool(
        name="work", bufs=3
    ) as work, tc.tile_pool(name="stats", bufs=5) as stats, tc.psum_pool(
        name="psum", bufs=1
    ) as psum, tc.manual_schedule():
        scalar_rows = slice(0, SCALAR_ROWS)
        vector_rows = slice(SCALAR_ROWS, PAIR * P)
        all_rows = slice(0, PAIR * P)
        live = {}

        def row_plane(width, name):
            plane = const.tile([P, width], BF16, name=name)
            nc.vector.memset(plane[:], 0.0)
            return plane

        def spread_row(out, plane):
            nc.tensor.matmul(out=out, lhsT=ones[:], rhs=plane[:], start=True, stop=True)

        def group_weight(copy, grouped, raw, cols):
            copy(
                out=grouped[:, cols, :].rearrange("p (c i) t -> p c t i", i=4),
                in_=raw[:, :, cols].rearrange("p t (c i) -> p c t i", i=4),
            )

        def quantise_weight(grouped, width, name):
            codes = const.tile([P, width], U32, name=name + "_codes", align_bytes=64)
            scales = const.tile([P, width], U8, name=name + "_scales", align_bytes=64)
            nc.vector.quantize_mx(
                out=codes[:].bitcast(FP8X4), scales=scales[:], in_=grouped[:].rearrange("p c t -> p (c t)")
            )
            return codes, scales

        eps = const.tile([P, 1], F32)
        nc.vector.memset(eps[:], EPS)
        bo_row = row_plane(D, "bo_row")
        warm = const.tile([P, 1], F32)
        nc.scalar.activation(out=warm[:], in_=eps[:], func=ACT.Abs_reciprocal_sqrt, bias=eps[:], scale=1.0)
        ones = const.tile([P, P], BF16)
        nc.vector.memset(ones[:], 1.0)
        g_row = row_plane(D, "g_row")
        b_row = row_plane(D, "b_row")
        b12_row = row_plane(2 * F, "b12_row")
        fln_rows = row_plane(P, "fln_rows")
        ident_f32 = const.tile([P, P], F32)
        make_identity(nc, ident_f32[:])
        ident_bf16 = const.tile([P, P], BF16)
        make_identity(nc, ident_bf16[:])

        def load(name, view, k):
            tile = inputs.tile([P, PAIR, D], BF16, tag=name)
            nc.sync.dma_start(out=tile[:], in_=view[:, PAIR * k : PAIR * (k + 1), :])
            live[name, k] = tile

        load("h", h_view, 0)
        nc.sync.dma_start(out=bo_row[0:1, :], in_=bo.unsqueeze(0))
        wo_raw = const.tile([P, PACK, D], BF16)
        for u in range(2):
            nc.sync.dma_start(
                out=wo_raw[:, 2 * u : 2 * u + 2, :],
                in_=Wo[256 * u : 256 * u + 256, :].rearrange("(q e) c -> q e c", e=2),
            )

        load("x", x_view, 0)
        load("h", h_view, 1)
        load("x", x_view, 1)
        nc.sync.dma_start(out=g_row[0:1, :], in_=ln2_g.unsqueeze(0))
        nc.sync.dma_start(out=b_row[0:1, :], in_=ln2_b.unsqueeze(0))
        load("h", h_view, 2)
        load("x", x_view, 2)
        w12_raw = const.tile([P, PACK, 2 * F], BF16)
        nc.sync.dma_start(out=fln_rows[0:PACK, :], in_=fln_g.rearrange("(t p) -> t p", p=P))
        nc.sync.dma_start(out=fln_rows[PACK : 2 * PACK, :], in_=fln_b.rearrange("(t p) -> t p", p=P))
        nc.sync.dma_start(out=w12_raw[:, :, 0:F], in_=W1.rearrange("(t p) f -> p t f", p=P))
        nc.sync.dma_start(out=w12_raw[:, :, F : 2 * F], in_=W2.rearrange("(t p) f -> p t f", p=P))
        nc.sync.dma_start(out=b12_row[0:1, 0:F], in_=b1.unsqueeze(0))
        nc.sync.dma_start(out=b12_row[0:1, F : 2 * F], in_=b2.unsqueeze(0))
        for k in range(3, PAIRS):
            load("h", h_view, k)
            load("x", x_view, k)

        bo_ps = psum.tile([P, D], F32, tag="nT1")
        spread_row(bo_ps[:], bo_row)
        bo_bc = const.tile([P, D], F32)
        wo_grouped = const.tile([P, D, PACK], BF16, align_bytes=64)

        def spread_ln2():
            g_bc = psum.tile([P, D], F32)
            spread_row(g_bc[:], g_row)
            b_bc = psum.tile([P, D], F32)
            spread_row(b_bc[:], b_row)
            live["g_bc"] = g_bc
            live["b_bc"] = b_bc

        def late_setup():
            b12_ps = psum.tile([P, 2 * F], F32, tag="acc2", bufs=ACC_BANKS["acc2"])
            spread_row(b12_ps[:], b12_row)
            b12_bc = const.tile([P, 2 * F], F32)
            nc.scalar.copy(out=b12_bc[:], in_=b12_ps[:])
            cols_ps = psum.tile([P, P], BF16, tag="nT0")
            nc.tensor.transpose(cols_ps[:], fln_rows[:], ident_bf16[:])
            fln_cols = const.tile([P, 2 * PACK], F32)
            nc.scalar.copy(out=fln_cols[:], in_=cols_ps[:, 0 : 2 * PACK])
            w12_grouped = const.tile([P, 2 * F, PACK], BF16, align_bytes=64)
            group_weight(nc.scalar.copy, w12_grouped, w12_raw, slice(0, 2 * F))
            live["w12_grouped"] = w12_grouped
            live["b12_bc"] = b12_bc
            live["fln_cols"] = fln_cols

        def quantise_w12():
            live["w12"] = quantise_weight(live["w12_grouped"], 2 * F, "w12")

        def add_bias(engine, bias, k):
            xb = work.tile([P, PAIR, D], F32, tag="xb", bufs=2)
            engine.tensor_tensor(
                out=xb[:], in0=live["x", k][:], in1=bias[:].unsqueeze(1).to_broadcast([P, PAIR, D]), op=ALU.add
            )
            live["xb", k] = xb

        def transpose_h(k):
            hT = psum.tile([P, PAIR, 2, P], F32, tag="hT")
            for j in range(PAIR):
                words = live["h", k][:, j, :].bitcast(F32)
                for u in range(2):
                    nc.tensor.transpose(hT[:, j, u, :], words[:, P * u : P * (u + 1)], ident_f32[:])
            live["hT", k] = hT

        def group_h(k):
            h_grouped = work.tile([P, PAIR * P, PACK], BF16, tag="h_grouped", align_bytes=64)
            nc.scalar.copy(
                out=h_grouped[:].bitcast(F32).rearrange("p (j r) u -> p j r u", j=PAIR),
                in_=live["hT", k][:].rearrange("p j u r -> p j r u"),
            )
            live["h_grouped", k] = h_grouped

        def quantise(name, k, rows=all_rows):
            if (name + "_codes", k) not in live:
                live[name + "_codes", k] = work.tile(
                    [P, PAIR * P], U32, tag=name + "_codes", name=name + "_codes", align_bytes=64
                )
                live[name + "_scales", k] = work.tile(
                    [P, PAIR * P], U8, tag=name + "_scales", name=name + "_scales", align_bytes=64
                )
            nc.vector.quantize_mx(
                out=live[name + "_codes", k][:, rows].bitcast(FP8X4),
                scales=live[name + "_scales", k][:, rows],
                in_=live[name + "_grouped", k][:, rows, :].rearrange("p r t -> p (r t)"),
            )

        def multiply(name, k, j, out, w_codes, w_scales):
            nc.tensor.matmul_mx(
                out=out,
                lhsT=live[name + "_codes", k][:, P * j : P * (j + 1)].bitcast(FP8X4),
                lhsT_scale=live[name + "_scales", k][:, P * j : P * (j + 1)],
                rhs=w_codes[:].bitcast(FP8X4),
                rhs_scale=w_scales[:],
                start=True,
                stop=True,
            )

        def project(k):
            for j in range(PAIR):
                acc = psum.tile([P, D], F32, tag="acc", bufs=ACC_BANKS["acc"])
                multiply("h", k, j, acc[:], live["wo"][0], live["wo"][1])
                live["acc", k, j] = acc

        def residual(k):
            y = work.tile([P, PAIR, D], F32, tag="y")
            for j in range(PAIR):
                nc.vector.scalar_tensor_tensor(
                    out=y[:, j, :],
                    in0=live["acc", k, j][:],
                    scalar=1.0,
                    in1=live["xb", k][:, j, :],
                    op0=ALU.mult,
                    op1=ALU.add,
                    accum_out=sums(k)[:, j : j + 1],
                )
            live["y", k] = y

        def sums(k):
            if ("sums", k) not in live:
                live["sums", k] = stats.tile([P, 2 * PAIR], F32, tag="sums", name="sums")
            return live["sums", k]

        def columns(k):
            return slice(0 if k < PAIRS else PAIR, 2 * PAIR if k >= LAG_R else PAIR)

        def means(k):
            neg_mean = stats.tile([P, 2 * PAIR], F32, tag="negmean")
            cols = columns(k)
            nc.scalar.mul(out=neg_mean[:, cols], in_=sums(k)[:, cols], mul=-1.0 / D)
            live["negmean", k] = neg_mean
            live["sumsq", k] = stats.tile([P, 2 * PAIR], F32, tag="sumsq", name="sumsq")

        def squares(name, k):
            pair, first = (k, 0) if name == "y" else (k - LAG_R, PAIR)
            if not 0 <= pair < PAIRS:
                return
            for j in range(PAIR):
                unread = work.tile([P, D], BF16, tag="squares", bufs=4)
                nc.scalar.activation(
                    out=unread[:],
                    in_=live[name, pair][:, j, :],
                    func=ACT.Square,
                    bias=live["negmean", k][:, first + j : first + j + 1],
                    scale=1.0,
                    accum_out=live["sumsq", k][:, first + j : first + j + 1],
                )

        def inverse_std(k):
            rstd = stats.tile([P, 2 * PAIR], F32, tag="rstd")
            cols = columns(k)
            nc.scalar.activation(
                out=rstd[:, cols], in_=live["sumsq", k][:, cols], func=ACT.Abs_reciprocal_sqrt, bias=eps[:], scale=1.0 / D
            )
            live["rstd", k] = rstd

        def statistic(which, name, k, j):
            kk, first = (k, 0) if name == "y" else (k + LAG_R, PAIR)
            return live[which, kk][:, first + j : first + j + 1]

        def first_norm(k):
            scaled = work.tile([P, PAIR, D], F32, tag="scaled", bufs=2)
            r = work.tile([P, PAIR, D], F32, tag="r", bufs=5)
            for j in range(PAIR):
                nc.vector.scalar_tensor_tensor(
                    out=scaled[:, j, :],
                    in0=live["y", k][:, j, :],
                    scalar=statistic("negmean", "y", k, j),
                    in1=live["g_bc"][:],
                    op0=ALU.add,
                    op1=ALU.mult,
                )
            for j in range(PAIR):
                nc.vector.scalar_tensor_tensor(
                    out=r[:, j, :],
                    in0=scaled[:, j, :],
                    scalar=statistic("rstd", "y", k, j),
                    in1=live["b_bc"][:],
                    op0=ALU.mult,
                    op1=ALU.add,
                    accum_out=sums(k + LAG_R)[:, PAIR + j : PAIR + j + 1],
                )
            nc.sync.dma_start(out=r_view[:, PAIR * k : PAIR * (k + 1), :], in_=r[:])
            live["r", k] = r

        def second_norm(engine, k):
            normed = work.tile([P, PAIR, D], F32, tag="normed", bufs=2)
            for j in range(PAIR):
                engine.tensor_scalar(
                    out=normed[:, j, :],
                    in0=live["r", k][:, j, :],
                    scalar1=statistic("negmean", "r", k, j),
                    scalar2=statistic("rstd", "r", k, j),
                    op0=ALU.add,
                    op1=ALU.mult,
                )
            live["normed", k] = normed

        def transpose_normed(k):
            for half in range(2):
                nT = psum.tile([P, 2, PAIR * P], F32, tag="nT%d" % half)
                for t in range(2):
                    cols = slice(P * (2 * half + t), P * (2 * half + t + 1))
                    for j in range(PAIR):
                        nc.tensor.transpose(nT[:, t, P * j : P * (j + 1)], live["normed", k][:, j, cols], ident_f32[:])
                live["nT", k, half] = nT

        def gain(k, planes=range(PACK), cols=all_rows):
            if ("h2T", k) not in live:
                live["h2T", k] = work.tile([P, PACK, PAIR * P], BF16, tag="h2T", name="h2T", bufs=2)
            for t in planes:
                nc.scalar.activation(
                    out=live["h2T", k][:, t, cols],
                    in_=live["nT", k, t // 2][:, t % 2, cols],
                    func=ACT.Identity,
                    bias=live["fln_cols"][:, PACK + t : PACK + t + 1],
                    scale=live["fln_cols"][:, t : t + 1],
                )

        def group_h2(copy, rows, k):
            if ("h2_grouped", k) not in live:
                live["h2_grouped", k] = work.tile(
                    [P, PAIR * P, PACK], BF16, tag="h2_grouped", name="h2_grouped", bufs=2, align_bytes=64
                )
            copy(
                out=live["h2_grouped", k][:, rows, :].rearrange("p (c i) t -> p c t i", i=4),
                in_=live["h2T", k][:, :, rows].rearrange("p t (c i) -> p c t i", i=4),
            )

        def project2(k, tiles=range(PAIR), tag="acc2"):
            if ("acc2", k) not in live:
                live["acc2", k] = psum.tile([P, PAIR, 2 * F], F32, tag=tag, name="acc2_" + tag, bufs=ACC_BANKS[tag])
            for j in tiles:
                multiply("h2", k, j, live["acc2", k][:, j, :], live["w12"][0], live["w12"][1])

        def bias2(k, tiles=range(PAIR)):
            first = (k * PAIR) % GROUP
            if first == 0 and tiles[0] == 0:
                live["out12"] = work.tile([P, 2, GROUP, F], F32, tag="out12", name="out12", bufs=2)
            out12 = live["out12"]
            own = slice(tiles[0], tiles[-1] + 1)
            nc.vector.tensor_tensor(
                out=out12[:, :, first + tiles[0] : first + tiles[-1] + 1, :].rearrange("p w j f -> p j w f"),
                in0=live["acc2", k][:, own, :].rearrange("p j (w f) -> p j w f", w=2),
                in1=live["b12_bc"][:].rearrange("p (w f) -> p w f", w=2).unsqueeze(1).to_broadcast([P, len(tiles), 2, F]),
                op=ALU.add,
            )
            if first + tiles[-1] + 1 == GROUP:
                group = slice(PAIR * (k + 1) - GROUP, PAIR * (k + 1))
                nc.sync.dma_start(out=g_view[:, group, :], in_=out12[:, 0, :, :])
                nc.sync.dma_start(out=hid_view[:, group, :], in_=out12[:, 1, :, :])

        def run(step, k, *args):
            if 0 <= k < PAIRS:
                step(*args, k)

        transpose_h(0)
        group_h(0)
        group_weight(nc.vector.tensor_copy, wo_grouped, wo_raw, slice(0, WO_SPLIT))
        group_weight(nc.scalar.copy, wo_grouped, wo_raw, slice(WO_SPLIT, D))
        transpose_h(1)
        quantise("h", 0)
        live["wo"] = quantise_weight(wo_grouped, D, "wo")
        nc.scalar.copy(out=bo_bc[:], in_=bo_ps[:])
        add_bias(nc.vector, bo_ps, 0)
        add_bias(nc.gpsimd, bo_bc, 1)
        group_h(1)
        project(0)
        spread_ln2()
        transpose_h(2)
        for i in range(PAIRS):
            if i == 2:
                late_setup()
            if i == 3:
                quantise_w12()
            run(second_norm, i - 3, nc.gpsimd)
            run(residual, i)
            if i <= 2:
                quantise("h", i + 1)
            if 0 <= i - 4:
                gain(i - 4, range(1, PACK))
            run(group_h, i + 2)
            run(means, i)
            run(group_h2, i - 4, nc.scalar.copy, scalar_rows)
            run(squares, i, "r")
            run(squares, i, "y")
            run(project, i + 1)
            run(transpose_h, i + 3)
            run(transpose_normed, i - 3)
            if 0 <= i - 3:
                gain(i - 3, range(0, 1))
            run(inverse_std, i)
            run(first_norm, i - 1)
            run(bias2, i - 5)
            run(add_bias, i + 2, nc.gpsimd, bo_bc)
            run(group_h2, i - 4, nc.vector.tensor_copy, vector_rows)
            if i >= 2:
                run(quantise, i + 2, "h")
            run(quantise, i - 4, "h2")
            run(project2, i - 4)
        n = PAIRS
        means(n)
        second_norm(nc.gpsimd, n - 3)
        gain(n - 4, range(1, PACK))
        first_norm(n - 1)
        transpose_normed(n - 3)
        squares("r", n)
        group_h2(nc.vector.tensor_copy, all_rows, n - 4)
        bias2(n - 5)
        quantise("h2", n - 4)
        project2(n - 4)
        gain(n - 3)
        inverse_std(n)
        means(n + 1)
        squares("r", n + 1)
        inverse_std(n + 1)
        second_norm(nc.vector, n - 2)
        transpose_normed(n - 2)
        group_h2(nc.vector.tensor_copy, all_rows, n - 3)
        second_norm(nc.vector, n - 1)
        gain(n - 2)
        transpose_normed(n - 1)
        bias2(n - 4)
        quantise("h2", n - 3)
        project2(n - 3, tag="acc")
        gain(n - 1, cols=slice(0, P))
        gain(n - 1, cols=slice(P, 2 * P))
        group_h2(nc.vector.tensor_copy, all_rows, n - 2)
        quantise("h2", n - 2)
        project2(n - 2, tag="acc")
        group_h2(nc.vector.tensor_copy, slice(0, P), n - 1)
        group_h2(nc.vector.tensor_copy, slice(P, 2 * P), n - 1)
        quantise("h2", n - 1, slice(0, P))
        project2(n - 1, range(0, 1))
        quantise("h2", n - 1, slice(P, 2 * P))
        project2(n - 1, range(1, 2))
        bias2(n - 3)
        bias2(n - 2)
        bias2(n - 1)
